import numpy as np
import ml_dtypes


def mxq(x, axis, fmt="e4m3"):
    dtype, down = {"e4m3": (ml_dtypes.float8_e4m3fn, 7), "e5m2": (ml_dtypes.float8_e5m2, 14)}[fmt]
    v = np.moveaxis(np.asarray(x, np.float32).astype(ml_dtypes.bfloat16).astype(np.float64), axis, -1)
    blocks = v.reshape(v.shape[:-1] + (-1, 32))
    amax = np.abs(blocks).max(-1, keepdims=True)
    byte = np.maximum(np.where(amax > 0, np.frexp(amax)[1] - 1 + 127, 0) - down, 1)
    scale = np.exp2(byte - 127.0)
    codes = (blocks / scale).astype(np.float32).astype(dtype).astype(np.float64)
    return np.moveaxis((codes * scale).reshape(v.shape), -1, axis)


WIDE = False


def mx_kscale(k):
    if not WIDE:
        return np.ones(k)
    levels = np.array([10, -10, 5, -5, 0])
    if k % 512:
        return np.exp2(np.random.permutation(np.resize(levels, k // 32))).repeat(32)
    a = np.empty((k // 512, 16))
    for p in range(k // 512):
        a[p, :8] = np.random.permutation(np.resize(levels, 8))
        for g in range(8):
            far = levels[np.abs(levels - a[p, g]) >= 10]
            a[p, g + 8] = far[np.random.randint(len(far))]
    return np.exp2(a.ravel()).repeat(32)


BF16 = ml_dtypes.bfloat16


def bf(x):
    return np.asarray(x, np.float32).astype(BF16)


def f64(x):
    return np.asarray(x).astype(np.float64)


B, L, D, O = 4, 128, 512, 32


def setup_inputs():
    s = mx_kscale(D)
    u = mx_kscale(D)
    w = np.random.standard_normal((O, D + 1, D))
    w[:, :D, :] *= 3.0 / D / s[:, None]
    w[:, D, :] *= 1.0 / np.sqrt(D)
    return {"x1": bf(np.random.standard_normal((B, L, D)) * s),
            "x2": bf(np.random.standard_normal((B, L, D)) / u),
            "bw": bf(np.random.uniform(size=(2,))),
            "W_bil": bf(w * u),
            "t_ones": bf(np.random.standard_normal((B, L, O))),
            "lin1": bf(np.random.standard_normal((B, L, O))),
            "lin2": bf(np.random.standard_normal((B, L, O))),
            "b_lin": bf(np.random.standard_normal(O) * 0.5)}


def reference(x1, x2, bw, W_bil, t_ones, lin1, lin2, b_lin):
    e = np.exp(f64(bw) - f64(bw).max())
    bwn = e / e.sum()
    w = f64(W_bil)
    t = (mxq(f64(x1).reshape(B * L, D), 1, "e4m3") @ mxq(w[:, :D, :], 1, "e4m3")) + w[:, D, :][:, None, :]
    t = t.reshape(O, B, L, D)
    pair = mxq(t, 3, "e4m3") @ mxq(f64(x2), 2, "e4m3").transpose(0, 2, 1)
    bil = pair.transpose(1, 2, 3, 0) + f64(t_ones)[:, :, None, :]
    lin = f64(lin1)[:, :, None, :] + f64(lin2)[:, None, :, :] + f64(b_lin)
    return bwn[0] * bil + bwn[1] * lin

from contextlib import ExitStack

import concourse.mybir as mybir
from concourse.masks import make_identity

B, L, D, O = 4, 128, 512, 32
FLOPS = 2 * B * L * D * D * O + 2 * O * B * L * L * D

F32 = mybir.dt.float32
BF16 = mybir.dt.bfloat16
U32 = mybir.dt.uint32
U8 = mybir.dt.uint8
FP8X4 = mybir.dt.float8_e4m3fn_x4
ALU = mybir.AluOpType
ACT = mybir.ActivationFunctionType

P = 128
PACK = 4
BANK_DT = F32
OGRP = 4
YH = 64
V_READ_EVERY = 64
W_BUFS = 5
MANUAL = False
V_COPY_Q = []


def tile_biaffine_pa_kernel(tc, x1, x2, bw, W_bil, t_ones, lin1, lin2, b_lin, out):
    nc = tc.nc
    with ExitStack() as ctx:
        keep = ctx.enter_context(tc.tile_pool(name="keep", bufs=1))
        work = ctx.enter_context(tc.tile_pool(name="work", bufs=2))
        psum = ctx.enter_context(tc.psum_pool(name="psum", bufs=8))
        if MANUAL:
            ctx.enter_context(tc.manual_schedule())

        bw_sb = keep.tile([P, 2], BF16, name="bw_sb", tag="bw_sb")
        nc.scalar.dma_start(out=bw_sb[:], in_=bw.partition_broadcast(P))
        bl_sb = keep.tile([P, O], BF16, name="bl_sb", tag="bl_sb")
        nc.scalar.dma_start(out=bl_sb[:], in_=b_lin.partition_broadcast(P))
        t1_sb = keep.tile([P, B, O], BF16, name="t1_sb", tag="t1_sb")
        nc.scalar.dma_start(out=t1_sb[:], in_=t_ones.rearrange("b x o -> x b o"))
        l1_sb = keep.tile([P, B, O], BF16, name="l1_sb", tag="l1_sb")
        nc.scalar.dma_start(out=l1_sb[:], in_=lin1.rearrange("b x o -> x b o"))

        ident = keep.tile([P, P], F32, name="ident", tag="ident")
        make_identity(nc, ident[:])

        x1c = keep.tile([P, B * L], U32, name="x1c", tag="x1c", align_bytes=64)
        x1s = keep.tile([P, B * L], U8, name="x1s", tag="x1s", align_bytes=64)
        x2c = keep.tile([P, B * L], U32, name="x2c", tag="x2c", align_bytes=64)
        x2s = keep.tile([P, B * L], U8, name="x2s", tag="x2s", align_bytes=64)
        tcod = keep.tile([P, O, B * L], U32, name="tcod", tag="tcod", align_bytes=64)
        tscl = keep.tile([P, O, B * L], U8, name="tscl", tag="tscl", align_bytes=64)

        wraw, wgrp, wq, banks, tbs, xts, tgs, biases, lin2bs = {}, {}, {}, {}, {}, {}, {}, {}, {}

        def load_tokens(x, key):
            raw = work.tile([P, B, D], BF16, name="xraw", tag="wraw", bufs=W_BUFS, align_bytes=64)
            for b in range(B):
                nc.sync.dma_start(out=raw[:, b, :], in_=x[b])
            tbs[key] = raw

        def load_w(o):
            raw = work.tile([P, PACK, D], BF16, name="wraw", tag="wraw", bufs=W_BUFS, align_bytes=64)
            nc.sync.dma_start(out=raw[:], in_=W_bil[o, 0:D, :].rearrange("(p s) j -> p s j", s=PACK))
            wraw[o] = raw

        def load_bias(c):
            bt = work.tile([P, OGRP, D], BF16, name="bias", tag="bias", bufs=2)
            nc.sync.dma_start(out=bt[:], in_=W_bil[c * OGRP : (c + 1) * OGRP, D, :].partition_broadcast(P))
            biases[c] = bt

        def load_lin2(b):
            l2 = work.tile([P, L, O], BF16, name="lin2b", tag="lin2b", bufs=4)
            nc.sync.dma_start(out=l2[:].rearrange("p y o -> p (y o)"), in_=lin2[b].rearrange("y o -> (y o)").partition_broadcast(P))
            lin2bs[b] = l2

        def interleave_w(o, copies):
            g = work.tile([P, D, PACK], BF16, name="wgrp", tag="wgrp", bufs=3, align_bytes=64)
            dst = g[:].rearrange("p (u c e) s -> p u c s e", u=2, e=2)
            src = wraw[o][:].rearrange("p s (c u e) -> p u c s e", u=2, e=2)
            for u in range(2):
                copies[u](out=dst[:, u], in_=src[:, u])
            wgrp[o] = g

        def quant_w(o):
            wc = work.tile([P, D], U32, name="wc", tag="wc", bufs=3, align_bytes=64)
            ws = work.tile([P, D], U8, name="ws", tag="ws", bufs=3, align_bytes=64)
            nc.vector.quantize_mx(out=wc[:].bitcast(FP8X4), scales=ws[:], in_=wgrp[o][:].rearrange("p j s -> p (j s)"))
            wq[o] = (wc, ws)

        def stage1(o):
            wc, ws = wq[o]
            banks[o] = []
            for b in range(B):
                cols = slice(b * L, (b + 1) * L)
                bank = psum.tile([P, D], BANK_DT, name="bank", tag="bank")
                nc.tensor.matmul_mx(
                    out=bank[:],
                    lhsT=x1c[:, cols].bitcast(FP8X4),
                    lhsT_scale=x1s[:, cols],
                    rhs=wc[:].bitcast(FP8X4),
                    rhs_scale=ws[:],
                    start=True,
                    stop=True,
                )
                banks[o].append(bank)

        def add_bias(o):
            tb = work.tile([P, B, D], BF16, name="tb", tag="tb", bufs=2, align_bytes=64)
            for b in range(B):
                nc.vector.tensor_tensor(
                    out=tb[:, b, :].rearrange("p (u c e) -> p u c e", u=2, e=2),
                    in0=banks[o][b][:].rearrange("p (u c e) -> p u c e", u=2, e=2),
                    in1=biases[o // OGRP][:, o % OGRP, :].rearrange("p (c u e) -> p u c e", u=2, e=2),
                    op=ALU.add,
                )
            tbs[o] = tb

        def transposes(key, permuted):
            words = tbs[key][:].bitcast(F32)
            xts[key] = []
            for q in range(2):
                xt = psum.tile([P, 2, 2, L], F32, name="xt", tag="bank")
                for h in range(2):
                    for u in range(2):
                        if permuted:
                            sel = words[:, 2 * q + h, u * P : (u + 1) * P]
                        else:
                            sel = words[:, 2 * q + h, u : D // 2 : 2]
                        nc.tensor.transpose(xt[:, h, u, :], sel, ident[:])
                xts[key].append(xt)

        def copy_out(key, v_q):
            tg = work.tile([P, B * L * PACK], BF16, name="tg", tag="tg", bufs=2, align_bytes=64)
            gw = tg[:].bitcast(F32).rearrange("p (b x u) -> p b x u", b=B, u=2)
            for q in range(2):
                src = xts[key][q][:].rearrange("p h u x -> p h x u")
                if q in v_q:
                    nc.vector.tensor_copy(out=gw[:, 2 * q : 2 * q + 2], in_=src)
                else:
                    nc.scalar.copy(out=gw[:, 2 * q : 2 * q + 2], in_=src)
            tgs[key] = tg

        def quant_tokens(key, codes, scales):
            nc.vector.quantize_mx(out=codes.bitcast(FP8X4), scales=scales, in_=tgs[key][:])

        load_tokens(x1, "x1")
        load_w(0)
        load_w(1)
        load_bias(0)
        load_tokens(x2, "x2")
        load_w(2)
        load_w(3)

        bwf = keep.tile([P, 2], F32, name="bwf", tag="bwf")
        nc.vector.tensor_copy(out=bwf[:], in_=bw_sb[:])
        bmax = keep.tile([P, 1], F32, name="bmax", tag="bmax")
        nc.vector.tensor_tensor(out=bmax[:], in0=bwf[:, 0:1], in1=bwf[:, 1:2], op=ALU.max)
        nmax = keep.tile([P, 1], F32, name="nmax", tag="nmax")
        nc.vector.tensor_scalar(out=nmax[:], in0=bmax[:], scalar1=-1.0, scalar2=None, op0=ALU.mult)
        bexp = keep.tile([P, 2], F32, name="bexp", tag="bexp")
        nc.scalar.activation(out=bexp[:], in_=bwf[:], func=ACT.Exp, bias=nmax[:], scale=1.0)
        bsum = keep.tile([P, 1], F32, name="bsum", tag="bsum")
        nc.vector.tensor_tensor(out=bsum[:], in0=bexp[:, 0:1], in1=bexp[:, 1:2], op=ALU.add)
        brec = keep.tile([P, 1], F32, name="brec", tag="brec")
        nc.vector.reciprocal(out=brec[:], in_=bsum[:])
        bwn = keep.tile([P, 2], F32, name="bwn", tag="bwn")
        nc.vector.tensor_scalar(out=bwn[:], in0=bexp[:], scalar1=brec[:], scalar2=None, op0=ALU.mult)

        lsum = keep.tile([P, B, O], F32, name="lsum", tag="lsum")
        nc.vector.tensor_tensor(out=lsum[:], in0=l1_sb[:], in1=bl_sb[:].unsqueeze(1).to_broadcast([P, B, O]), op=ALU.add)
        lscl = keep.tile([P, B * O], F32, name="lscl", tag="lscl")
        nc.vector.tensor_scalar(out=lscl[:], in0=lsum[:].rearrange("p b o -> p (b o)"), scalar1=bwn[:, 1:2], scalar2=None, op0=ALU.mult)
        xterm = keep.tile([P, B * O], F32, name="xterm", tag="xterm")
        nc.vector.scalar_tensor_tensor(out=xterm[:], in0=t1_sb[:].rearrange("p b o -> p (b o)"), scalar=bwn[:, 0:1], in1=lscl[:], op0=ALU.mult, op1=ALU.add)

        transposes("x1", False)
        copy_out("x1", [1])
        interleave_w(0, [nc.scalar.copy, nc.vector.tensor_copy])
        quant_tokens("x1", x1c[:], x1s[:])
        transposes("x2", False)
        copy_out("x2", [0, 1])
        quant_w(0)
        interleave_w(1, [nc.scalar.copy, nc.scalar.copy])
        quant_tokens("x2", x2c[:], x2s[:])
        stage1(0)
        interleave_w(2, [nc.scalar.copy, nc.scalar.copy])
        quant_w(1)

        for i in range(O + 1):
            if 4 <= i + 4 < O:
                load_w(i + 4)
            if (i + 2) % OGRP == 0 and (i + 2) // OGRP < O // OGRP:
                load_bias((i + 2) // OGRP)
            if O - 16 <= i < O and i % 4 == 0:
                load_lin2((i - (O - 16)) // 4)
            if 0 <= i - 1:
                copy_out(i - 1, V_COPY_Q)
            if i + 3 < O:
                interleave_w(i + 3, [nc.scalar.copy, nc.scalar.copy])
            if i + 1 < O:
                stage1(i + 1)
            if i < O:
                add_bias(i)
                transposes(i, True)
            if i + 2 < O:
                quant_w(i + 2)
            if 0 <= i - 1:
                quant_tokens(i - 1, tcod[:, i - 1, :], tscl[:, i - 1, :])

        def add_lin2(b, stage, tmps, g, ysl):
            osl = slice(g * OGRP, (g + 1) * OGRP)
            nc.vector.scalar_tensor_tensor(
                out=stage[:, ysl, osl],
                in0=lin2bs[b][:, ysl, osl],
                scalar=bwn[:, 1:2],
                in1=tmps[g][:, :, ysl].rearrange("p k y -> p y k"),
                op0=ALU.mult,
                op1=ALU.add,
            )

        for b in range(B):
            cols = slice(b * L, (b + 1) * L)
            stage = work.tile([P, L, O], F32, name="stage", tag="stage", bufs=2)
            tmps = []
            for g in range(O // OGRP):
                pb = psum.tile([P, OGRP, L], F32, name="pair", tag="bank")
                for k in range(OGRP):
                    o = g * OGRP + k
                    nc.tensor.matmul_mx(
                        out=pb[:, k, :],
                        lhsT=tcod[:, o, cols].bitcast(FP8X4),
                        lhsT_scale=tscl[:, o, cols],
                        rhs=x2c[:, cols].bitcast(FP8X4),
                        rhs_scale=x2s[:, cols],
                        start=True,
                        stop=True,
                    )
                tmp = work.tile([P, OGRP, L], F32, name="tmp", tag="tmp", bufs=8)
                for k in range(OGRP):
                    o = g * OGRP + k
                    xcol = xterm[:, b * O + o : b * O + o + 1]
                    if o % V_READ_EVERY == V_READ_EVERY - 1:
                        nc.vector.tensor_scalar(out=tmp[:, k, :], in0=pb[:, k, :], scalar1=bwn[:, 0:1], scalar2=xcol, op0=ALU.mult, op1=ALU.add)
                    else:
                        nc.scalar.activation(out=tmp[:, k, :], in_=pb[:, k, :], func=ACT.Identity, bias=xcol, scale=bwn[:, 0:1])
                tmps.append(tmp)
                if b < B - 1:
                    add_lin2(b, stage, tmps, g, slice(0, L))
            if b < B - 1:
                nc.sync.dma_start(out=out[b], in_=stage[:])
            else:
                for y0 in range(0, L, YH):
                    ysl = slice(y0, y0 + YH)
                    for g in range(O // OGRP):
                        add_lin2(b, stage, tmps, g, ysl)
                    nc.sync.dma_start(out=out[b, :, ysl, :], in_=stage[:, ysl, :])
